import numpy as np
import ml_dtypes


def mxq(x, axis, fmt="e4m3"):
    dtype, down = {"e4m3": (ml_dtypes.float8_e4m3fn, 7), "e5m2": (ml_dtypes.float8_e5m2, 14)}[fmt]
    v = np.moveaxis(np.asarray(x, np.float32).astype(ml_dtypes.bfloat16).astype(np.float64), axis, -1)
    blocks = v.reshape(v.shape[:-1] + (-1, 32))
    amax = np.abs(blocks).max(-1, keepdims=True)
    byte = np.maximum(np.where(amax > 0, np.frexp(amax)[1] - 1 + 127, 0) - down, 1)
    scale = np.exp2(byte - 127.0)
    codes = (blocks / scale).astype(np.float32).astype(dtype).astype(np.float64)
    return np.moveaxis((codes * scale).reshape(v.shape), -1, axis)


WIDE = False


def mx_kscale(k):
    if not WIDE:
        return np.ones(k)
    levels = np.array([10, -10, 5, -5, 0])
    a = np.random.permutation(np.resize(levels, k // 512 * 4)).reshape(k // 512, 4)
    idx = np.arange(k)
    return np.exp2(a[idx // 512, idx % 128 // 32])


BF16 = ml_dtypes.bfloat16


def bf(x):
    return np.asarray(x, np.float32).astype(BF16)


def f64(x):
    return np.asarray(x).astype(np.float64)


B, IN_C, OUT_C, H, W, K, STRIDE, PAD = 32, 512, 128, 2, 2, 3, 1, 1
OH = (H + 2 * PAD - K) // STRIDE + 1
OW = (W + 2 * PAD - K) // STRIDE + 1


def _span(t, n_in, n_out):
    lo = max(0, -((t - PAD) // STRIDE))
    hi = min(n_out, (n_in - 1 + PAD - t) // STRIDE + 1)
    return lo, hi


def setup_inputs():
    s = mx_kscale(IN_C)
    x = np.random.standard_normal((B, IN_C, H, W)) * s[None, :, None, None]
    weights = np.random.uniform(0.0, 1.0, (OH, OW, OUT_C, IN_C, K, K)) * (1.7 / np.sqrt(IN_C * K * K)) / s[None, None, None, :, None, None]
    bias = np.random.uniform(0.0, 1.0, (OUT_C, OH, OW))
    return {"x": bf(x), "weights": bf(weights), "bias": bf(bias)}


def reference(x, weights, bias):
    xq = mxq(f64(x), 1, "e4m3")
    wf = f64(weights)
    acc = np.zeros((OH, OW, B, OUT_C))
    for i in range(K):
        h0, h1 = _span(i, H, OH)
        for j in range(K):
            w0, w1 = _span(j, W, OW)
            xs = xq[:, :, h0 * STRIDE + i - PAD:(h1 - 1) * STRIDE + i - PAD + 1:STRIDE,
                    w0 * STRIDE + j - PAD:(w1 - 1) * STRIDE + j - PAD + 1:STRIDE]
            wq = mxq(wf[h0:h1, w0:w1, :, :, i, j], 3, "e4m3")
            acc[h0:h1, w0:w1] += xs.transpose(2, 3, 0, 1) @ wq.transpose(0, 1, 3, 2)
    return acc.transpose(2, 3, 0, 1) + f64(bias)[None]

@@ -1,0 +1,128 @@
+from contextlib import ExitStack
+
+import concourse.mybir as mybir
+from concourse.masks import make_identity
+
+BF16 = mybir.dt.bfloat16
+F32 = mybir.dt.float32
+U32 = mybir.dt.uint32
+U8 = mybir.dt.uint8
+FP8X4 = mybir.dt.float8_e4m3fn_x4
+
+P = 128
+PACK = 4
+BATCH = 32
+CHANNELS = P * PACK
+OUT_CH = 128
+SIDE = 2
+TAPS = 3
+PIXELS = SIDE * SIDE
+LOCATIONS = SIDE * SIDE
+O_LOAD = P // PACK
+O_UNIT = 64
+LOADS_PER_UNIT = O_UNIT // O_LOAD
+UNITS_PER_LOCATION = OUT_CH // O_UNIT
+UNITS = LOCATIONS * UNITS_PER_LOCATION
+COPIES = P // BATCH
+
+FLOPS = 2 * BATCH * OUT_CH * LOCATIONS * PIXELS * CHANNELS
+BYTES = (
+    2 * BATCH * CHANNELS * PIXELS
+    + 2 * LOCATIONS * OUT_CH * CHANNELS * PIXELS
+    + 2 * OUT_CH * LOCATIONS
+    + 4 * BATCH * OUT_CH * LOCATIONS
+)
+
+
+def tile_locallyconnected2d_s_kernel(tc, x, weights, bias, out):
+    nc = tc.nc
+    with ExitStack() as stack:
+        keep = stack.enter_context(tc.tile_pool(name="keep", bufs=1))
+        w_pool = stack.enter_context(tc.tile_pool(name="w_pool", bufs=UNITS * LOADS_PER_UNIT))
+        stage = stack.enter_context(tc.tile_pool(name="stage", bufs=6))
+        psum_t = stack.enter_context(tc.psum_pool(name="psum_t", bufs=6))
+        psum_x = stack.enter_context(tc.psum_pool(name="psum_x", bufs=1))
+        psum_acc = stack.enter_context(tc.psum_pool(name="psum_acc", bufs=1))
+
+        x_raw = keep.tile([P, P, PIXELS], BF16)
+        nc.scalar.dma_start(
+            out=x_raw[:], in_=x.rearrange("b (t c) y z -> (b t) c (y z)", t=PACK)
+        )
+        bias_rows = keep.tile([BATCH, OUT_CH, LOCATIONS], BF16)
+        nc.scalar.dma_start(
+            out=bias_rows[:].rearrange("b o l -> b (o l)"),
+            in_=bias.rearrange("o h w -> (o h w)").partition_broadcast(BATCH),
+        )
+        w_loads = weights.rearrange(
+            "h w (g o) (t c) i j -> (h w g) (o t) c i j", o=O_LOAD, t=PACK
+        )
+        w_raw = []
+        for n in range(UNITS * LOADS_PER_UNIT):
+            w_tile = w_pool.tile([P, P, TAPS, TAPS], BF16, name="w_tile")
+            nc.sync.dma_start(out=w_tile[:], in_=w_loads[n])
+            w_raw.append(w_tile)
+
+        identity = keep.tile([P, P], BF16)
+        make_identity(nc, identity[:])
+
+        x_t = psum_x.tile([P, PIXELS, P], BF16)
+        for q in range(PIXELS):
+            nc.tensor.transpose(x_t[:, q, :], x_raw[:, :, q], identity[:])
+        x_grouped = keep.tile([P, PIXELS, COPIES, P], BF16, align_bytes=64)
+        nc.vector.tensor_copy(
+            out=x_grouped[:],
+            in_=x_t[:].unsqueeze(2).to_broadcast([P, PIXELS, COPIES, P]),
+        )
+        x_codes = keep.tile([P, PIXELS, P], U32, align_bytes=64)
+        x_scales = keep.tile([P, PIXELS, P], U8, align_bytes=64)
+        nc.vector.quantize_mx(
+            out=x_codes[:].rearrange("p q m -> p (q m)").bitcast(FP8X4),
+            scales=x_scales[:].rearrange("p q m -> p (q m)"),
+            in_=x_grouped[:].rearrange("p q r m -> p (q r m)"),
+        )
+
+        w_codes = keep.tile([P, PIXELS, LOCATIONS, OUT_CH], U32, align_bytes=64)
+        w_scales = keep.tile([P, PIXELS, LOCATIONS, OUT_CH], U8, align_bytes=64)
+        acc = psum_acc.tile([P, LOCATIONS, OUT_CH], F32)
+
+        for loc in range(LOCATIONS):
+            h, w = divmod(loc, SIDE)
+            for half in range(UNITS_PER_LOCATION):
+                o_cols = slice(half * O_UNIT, (half + 1) * O_UNIT)
+                for q in range(PIXELS):
+                    y, z = divmod(q, SIDE)
+                    w_t = psum_t.tile([P, LOADS_PER_UNIT, P], BF16)
+                    for s in range(LOADS_PER_UNIT):
+                        w_tile = w_raw[(loc * UNITS_PER_LOCATION + half) * LOADS_PER_UNIT + s]
+                        nc.tensor.transpose(
+                            w_t[:, s, :], w_tile[:, :, y - h + 1, z - w + 1], identity[:]
+                        )
+                    w_grouped = stage.tile([P, O_UNIT * PACK], BF16, align_bytes=64)
+                    nc.scalar.copy(out=w_grouped[:], in_=w_t[:].rearrange("p s m -> p (s m)"))
+                    nc.vector.quantize_mx(
+                        out=w_codes[:, q, loc, o_cols].bitcast(FP8X4),
+                        scales=w_scales[:, q, loc, o_cols],
+                        in_=w_grouped[:],
+                    )
+            for q in range(PIXELS):
+                nc.tensor.matmul_mx(
+                    out=acc[:, loc, :],
+                    lhsT=x_codes[:, q, :].bitcast(FP8X4),
+                    lhsT_scale=x_scales[:, q, :],
+                    rhs=w_codes[:, q, loc, :].bitcast(FP8X4),
+                    rhs_scale=w_scales[:, q, loc, :],
+                    start=(q == 0),
+                    stop=(q == PIXELS - 1),
+                )
+
+        result = keep.tile([BATCH, OUT_CH, LOCATIONS], F32)
+        nc.vector.tensor_tensor(
+            out=result[:],
+            in0=acc[0:BATCH].rearrange("b l o -> b o l"),
+            in1=bias_rows[:],
+            op=mybir.AluOpType.add,
+        )
+        nc.sync.dma_start(
+            out=out.rearrange("b o h w -> b (o h w)"),
+            in_=result[:].rearrange("b o l -> b (o l)"),
+        )

@@ -11,19 +11,21 @@ FP8X4 = mybir.dt.float8_e4m3fn_x4
 
 P = 128
 PACK = 4
+PAIR = 2
 BATCH = 32
 CHANNELS = P * PACK
+HALVES = PACK // PAIR
+C_HALF = CHANNELS // HALVES
 OUT_CH = 128
 SIDE = 2
 TAPS = 3
 PIXELS = SIDE * SIDE
 LOCATIONS = SIDE * SIDE
-O_LOAD = P // PACK
-O_UNIT = 64
-LOADS_PER_UNIT = O_UNIT // O_LOAD
+O_UNIT = P // HALVES
 UNITS_PER_LOCATION = OUT_CH // O_UNIT
 UNITS = LOCATIONS * UNITS_PER_LOCATION
-COPIES = P // BATCH
+X_LOADS = P // (BATCH * HALVES)
+X_REPEATS = P // (X_LOADS * BATCH)
 
 FLOPS = 2 * BATCH * OUT_CH * LOCATIONS * PIXELS * CHANNELS
 BYTES = (
@@ -38,40 +40,44 @@ def tile_locallyconnected2d_s_kernel(tc, x, weights, bias, out):
     nc = tc.nc
     with ExitStack() as stack:
         keep = stack.enter_context(tc.tile_pool(name="keep", bufs=1))
-        w_pool = stack.enter_context(tc.tile_pool(name="w_pool", bufs=UNITS * LOADS_PER_UNIT))
-        stage = stack.enter_context(tc.tile_pool(name="stage", bufs=6))
+        w_pool = stack.enter_context(tc.tile_pool(name="w_pool", bufs=UNITS))
+        stage = stack.enter_context(tc.tile_pool(name="stage", bufs=4))
         psum_t = stack.enter_context(tc.psum_pool(name="psum_t", bufs=6))
         psum_x = stack.enter_context(tc.psum_pool(name="psum_x", bufs=1))
         psum_acc = stack.enter_context(tc.psum_pool(name="psum_acc", bufs=1))
 
-        x_raw = keep.tile([P, P, PIXELS], BF16)
-        nc.scalar.dma_start(
-            out=x_raw[:], in_=x.rearrange("b (t c) y z -> (b t) c (y z)", t=PACK)
-        )
+        x_raw = keep.tile([P, C_HALF, PIXELS], BF16)
+        x_rows = x.rearrange("b (u c) y z -> (b u) c (y z)", u=HALVES)
+        for r in range(X_LOADS):
+            nc.scalar.dma_start(
+                out=x_raw[r * BATCH * HALVES : (r + 1) * BATCH * HALVES], in_=x_rows
+            )
         bias_rows = keep.tile([BATCH, OUT_CH, LOCATIONS], BF16)
         nc.scalar.dma_start(
             out=bias_rows[:].rearrange("b o l -> b (o l)"),
             in_=bias.rearrange("o h w -> (o h w)").partition_broadcast(BATCH),
         )
         w_loads = weights.rearrange(
-            "h w (g o) (t c) i j -> (h w g) (o t) c i j", o=O_LOAD, t=PACK
+            "h w (g o) (u c) i j -> (h w g) (o u) c i j", o=O_UNIT, u=HALVES
         )
         w_raw = []
-        for n in range(UNITS * LOADS_PER_UNIT):
-            w_tile = w_pool.tile([P, P, TAPS, TAPS], BF16, name="w_tile")
+        for n in range(UNITS):
+            w_tile = w_pool.tile([P, C_HALF, TAPS, TAPS], BF16, name="w_tile")
             nc.sync.dma_start(out=w_tile[:], in_=w_loads[n])
             w_raw.append(w_tile)
 
-        identity = keep.tile([P, P], BF16)
+        identity = keep.tile([P, P], F32)
         make_identity(nc, identity[:])
 
-        x_t = psum_x.tile([P, PIXELS, P], BF16)
+        x_sorted = keep.tile([P, PIXELS, C_HALF], BF16)
+        nc.vector.tensor_copy(out=x_sorted[:], in_=x_raw[:].rearrange("p c q -> p q c"))
+        x_t = psum_x.tile([P, PIXELS, P], F32)
         for q in range(PIXELS):
-            nc.tensor.transpose(x_t[:, q, :], x_raw[:, :, q], identity[:])
-        x_grouped = keep.tile([P, PIXELS, COPIES, P], BF16, align_bytes=64)
+            nc.tensor.transpose(x_t[:, q, :], x_sorted[:, q, :].bitcast(F32), identity[:])
+        x_grouped = keep.tile([P, PIXELS, X_REPEATS, P * PAIR], BF16, align_bytes=64)
         nc.vector.tensor_copy(
-            out=x_grouped[:],
-            in_=x_t[:].unsqueeze(2).to_broadcast([P, PIXELS, COPIES, P]),
+            out=x_grouped[:].bitcast(F32),
+            in_=x_t[:].unsqueeze(2).to_broadcast([P, PIXELS, X_REPEATS, P]),
         )
         x_codes = keep.tile([P, PIXELS, P], U32, align_bytes=64)
         x_scales = keep.tile([P, PIXELS, P], U8, align_bytes=64)
@@ -88,22 +94,25 @@ def tile_locallyconnected2d_s_kernel(tc, x, weights, bias, out):
         for loc in range(LOCATIONS):
             h, w = divmod(loc, SIDE)
             for half in range(UNITS_PER_LOCATION):
+                w_tile = w_raw[loc * UNITS_PER_LOCATION + half]
                 o_cols = slice(half * O_UNIT, (half + 1) * O_UNIT)
-                for q in range(PIXELS):
-                    y, z = divmod(q, SIDE)
-                    w_t = psum_t.tile([P, LOADS_PER_UNIT, P], BF16)
-                    for s in range(LOADS_PER_UNIT):
-                        w_tile = w_raw[(loc * UNITS_PER_LOCATION + half) * LOADS_PER_UNIT + s]
-                        nc.tensor.transpose(
-                            w_t[:, s, :], w_tile[:, :, y - h + 1, z - w + 1], identity[:]
-                        )
-                    w_grouped = stage.tile([P, O_UNIT * PACK], BF16, align_bytes=64)
-                    nc.scalar.copy(out=w_grouped[:], in_=w_t[:].rearrange("p s m -> p (s m)"))
-                    nc.vector.quantize_mx(
-                        out=w_codes[:, q, loc, o_cols].bitcast(FP8X4),
-                        scales=w_scales[:, q, loc, o_cols],
-                        in_=w_grouped[:],
+                for y in range(SIDE):
+                    w_sorted = stage.tile([P, SIDE, C_HALF], BF16)
+                    nc.vector.tensor_copy(
+                        out=w_sorted[:].rearrange("p z c -> p c z"),
+                        in_=w_tile[:, :, y - h + 1, 1 - w : 1 - w + SIDE],
                     )
+                    for z in range(SIDE):
+                        q = y * SIDE + z
+                        w_t = psum_t.tile([P, P], F32)
+                        nc.tensor.transpose(w_t[:], w_sorted[:, z, :].bitcast(F32), identity[:])
+                        w_grouped = stage.tile([P, O_UNIT * PACK], BF16, align_bytes=64)
+                        nc.scalar.copy(out=w_grouped[:].bitcast(F32), in_=w_t[:])
+                        nc.vector.quantize_mx(
+                            out=w_codes[:, q, loc, o_cols].bitcast(FP8X4),
+                            scales=w_scales[:, q, loc, o_cols],
+                            in_=w_grouped[:],
+                        )
             for q in range(PIXELS):
                 nc.tensor.matmul_mx(
                     out=acc[:, loc, :],

@@ -11,21 +11,19 @@ FP8X4 = mybir.dt.float8_e4m3fn_x4
 
 P = 128
 PACK = 4
-PAIR = 2
 BATCH = 32
 CHANNELS = P * PACK
-HALVES = PACK // PAIR
-C_HALF = CHANNELS // HALVES
 OUT_CH = 128
 SIDE = 2
 TAPS = 3
 PIXELS = SIDE * SIDE
 LOCATIONS = SIDE * SIDE
-O_UNIT = P // HALVES
+O_LOAD = P // PACK
+O_UNIT = 64
+LOADS_PER_UNIT = O_UNIT // O_LOAD
 UNITS_PER_LOCATION = OUT_CH // O_UNIT
 UNITS = LOCATIONS * UNITS_PER_LOCATION
-X_LOADS = P // (BATCH * HALVES)
-X_REPEATS = P // (X_LOADS * BATCH)
+COPIES = P // BATCH
 
 FLOPS = 2 * BATCH * OUT_CH * LOCATIONS * PIXELS * CHANNELS
 BYTES = (
@@ -40,44 +38,40 @@ def tile_locallyconnected2d_s_kernel(tc, x, weights, bias, out):
     nc = tc.nc
     with ExitStack() as stack:
         keep = stack.enter_context(tc.tile_pool(name="keep", bufs=1))
-        w_pool = stack.enter_context(tc.tile_pool(name="w_pool", bufs=UNITS))
-        stage = stack.enter_context(tc.tile_pool(name="stage", bufs=4))
+        w_pool = stack.enter_context(tc.tile_pool(name="w_pool", bufs=UNITS * LOADS_PER_UNIT))
+        stage = stack.enter_context(tc.tile_pool(name="stage", bufs=6))
         psum_t = stack.enter_context(tc.psum_pool(name="psum_t", bufs=6))
         psum_x = stack.enter_context(tc.psum_pool(name="psum_x", bufs=1))
         psum_acc = stack.enter_context(tc.psum_pool(name="psum_acc", bufs=1))
 
-        x_raw = keep.tile([P, C_HALF, PIXELS], BF16)
-        x_rows = x.rearrange("b (u c) y z -> (b u) c (y z)", u=HALVES)
-        for r in range(X_LOADS):
-            nc.scalar.dma_start(
-                out=x_raw[r * BATCH * HALVES : (r + 1) * BATCH * HALVES], in_=x_rows
-            )
+        x_raw = keep.tile([P, P, PIXELS], BF16)
+        nc.scalar.dma_start(
+            out=x_raw[:], in_=x.rearrange("b (t c) y z -> (b t) c (y z)", t=PACK)
+        )
         bias_rows = keep.tile([BATCH, OUT_CH, LOCATIONS], BF16)
         nc.scalar.dma_start(
             out=bias_rows[:].rearrange("b o l -> b (o l)"),
             in_=bias.rearrange("o h w -> (o h w)").partition_broadcast(BATCH),
         )
         w_loads = weights.rearrange(
-            "h w (g o) (u c) i j -> (h w g) (o u) c i j", o=O_UNIT, u=HALVES
+            "h w (g o) (t c) i j -> (h w g) (o t) c i j", o=O_LOAD, t=PACK
         )
         w_raw = []
-        for n in range(UNITS):
-            w_tile = w_pool.tile([P, C_HALF, TAPS, TAPS], BF16, name="w_tile")
+        for n in range(UNITS * LOADS_PER_UNIT):
+            w_tile = w_pool.tile([P, P, TAPS, TAPS], BF16, name="w_tile")
             nc.sync.dma_start(out=w_tile[:], in_=w_loads[n])
             w_raw.append(w_tile)
 
-        identity = keep.tile([P, P], F32)
+        identity = keep.tile([P, P], BF16)
         make_identity(nc, identity[:])
 
-        x_sorted = keep.tile([P, PIXELS, C_HALF], BF16)
-        nc.vector.tensor_copy(out=x_sorted[:], in_=x_raw[:].rearrange("p c q -> p q c"))
-        x_t = psum_x.tile([P, PIXELS, P], F32)
+        x_t = psum_x.tile([P, PIXELS, P], BF16)
         for q in range(PIXELS):
-            nc.tensor.transpose(x_t[:, q, :], x_sorted[:, q, :].bitcast(F32), identity[:])
-        x_grouped = keep.tile([P, PIXELS, X_REPEATS, P * PAIR], BF16, align_bytes=64)
-        nc.vector.tensor_copy(
-            out=x_grouped[:].bitcast(F32),
-            in_=x_t[:].unsqueeze(2).to_broadcast([P, PIXELS, X_REPEATS, P]),
+            nc.tensor.transpose(x_t[:, q, :], x_raw[:, :, q], identity[:])
+        x_grouped = keep.tile([P, PIXELS, COPIES, P], BF16, align_bytes=64)
+        nc.scalar.copy(
+            out=x_grouped[:],
+            in_=x_t[:].unsqueeze(2).to_broadcast([P, PIXELS, COPIES, P]),
         )
         x_codes = keep.tile([P, PIXELS, P], U32, align_bytes=64)
         x_scales = keep.tile([P, PIXELS, P], U8, align_bytes=64)
@@ -94,25 +88,28 @@ def tile_locallyconnected2d_s_kernel(tc, x, weights, bias, out):
         for loc in range(LOCATIONS):
             h, w = divmod(loc, SIDE)
             for half in range(UNITS_PER_LOCATION):
-                w_tile = w_raw[loc * UNITS_PER_LOCATION + half]
                 o_cols = slice(half * O_UNIT, (half + 1) * O_UNIT)
-                for y in range(SIDE):
-                    w_sorted = stage.tile([P, SIDE, C_HALF], BF16)
+                w_picked = stage.tile([P, LOADS_PER_UNIT, SIDE, P, SIDE], BF16)
+                for s in range(LOADS_PER_UNIT):
+                    w_tile = w_raw[(loc * UNITS_PER_LOCATION + half) * LOADS_PER_UNIT + s]
                     nc.vector.tensor_copy(
-                        out=w_sorted[:].rearrange("p z c -> p c z"),
-                        in_=w_tile[:, :, y - h + 1, 1 - w : 1 - w + SIDE],
+                        out=w_picked[:, s],
+                        in_=w_tile[:, :, 1 - h : 1 - h + SIDE, 1 - w : 1 - w + SIDE].rearrange(
+                            "p c y z -> p y c z"
+                        ),
                     )
-                    for z in range(SIDE):
-                        q = y * SIDE + z
-                        w_t = psum_t.tile([P, P], F32)
-                        nc.tensor.transpose(w_t[:], w_sorted[:, z, :].bitcast(F32), identity[:])
-                        w_grouped = stage.tile([P, O_UNIT * PACK], BF16, align_bytes=64)
-                        nc.scalar.copy(out=w_grouped[:].bitcast(F32), in_=w_t[:])
-                        nc.vector.quantize_mx(
-                            out=w_codes[:, q, loc, o_cols].bitcast(FP8X4),
-                            scales=w_scales[:, q, loc, o_cols],
-                            in_=w_grouped[:],
-                        )
+                for q in range(PIXELS):
+                    y, z = divmod(q, SIDE)
+                    w_t = psum_t.tile([P, LOADS_PER_UNIT, P], BF16)
+                    for s in range(LOADS_PER_UNIT):
+                        nc.tensor.transpose(w_t[:, s, :], w_picked[:, s, y, :, z], identity[:])
+                    w_grouped = stage.tile([P, O_UNIT * PACK], BF16, align_bytes=64)
+                    nc.scalar.copy(out=w_grouped[:], in_=w_t[:].rearrange("p s m -> p (s m)"))
+                    nc.vector.quantize_mx(
+                        out=w_codes[:, q, loc, o_cols].bitcast(FP8X4),
+                        scales=w_scales[:, q, loc, o_cols],
+                        in_=w_grouped[:],
+                    )
             for q in range(PIXELS):
                 nc.tensor.matmul_mx(
                     out=acc[:, loc, :],

@@ -11,19 +11,19 @@ FP8X4 = mybir.dt.float8_e4m3fn_x4
 
 P = 128
 PACK = 4
+PAIR = 2
 BATCH = 32
 CHANNELS = P * PACK
+HALVES = PACK // PAIR
+C_HALF = CHANNELS // HALVES
 OUT_CH = 128
 SIDE = 2
 TAPS = 3
 PIXELS = SIDE * SIDE
 LOCATIONS = SIDE * SIDE
-O_LOAD = P // PACK
-O_UNIT = 64
-LOADS_PER_UNIT = O_UNIT // O_LOAD
-UNITS_PER_LOCATION = OUT_CH // O_UNIT
-UNITS = LOCATIONS * UNITS_PER_LOCATION
-COPIES = P // BATCH
+X_LOADS = P // (BATCH * HALVES)
+X_REPEATS = P // (X_LOADS * BATCH)
+C_VECTOR = 3 * C_HALF // 4
 
 FLOPS = 2 * BATCH * OUT_CH * LOCATIONS * PIXELS * CHANNELS
 BYTES = (
@@ -38,88 +38,121 @@ def tile_locallyconnected2d_s_kernel(tc, x, weights, bias, out):
     nc = tc.nc
     with ExitStack() as stack:
         keep = stack.enter_context(tc.tile_pool(name="keep", bufs=1))
-        w_pool = stack.enter_context(tc.tile_pool(name="w_pool", bufs=UNITS * LOADS_PER_UNIT))
-        stage = stack.enter_context(tc.tile_pool(name="stage", bufs=6))
-        psum_t = stack.enter_context(tc.psum_pool(name="psum_t", bufs=6))
+        w_pool = stack.enter_context(tc.tile_pool(name="w_pool", bufs=LOCATIONS * HALVES))
+        stage = stack.enter_context(tc.tile_pool(name="stage", bufs=4))
+        psum_t = stack.enter_context(tc.psum_pool(name="psum_t", bufs=2 * SIDE))
         psum_x = stack.enter_context(tc.psum_pool(name="psum_x", bufs=1))
         psum_acc = stack.enter_context(tc.psum_pool(name="psum_acc", bufs=1))
+        stack.enter_context(tc.manual_schedule())
 
-        x_raw = keep.tile([P, P, PIXELS], BF16)
-        nc.scalar.dma_start(
-            out=x_raw[:], in_=x.rearrange("b (t c) y z -> (b t) c (y z)", t=PACK)
-        )
+        x_raw = keep.tile([P, C_HALF, PIXELS], BF16)
+        x_rows = x.rearrange("b (u c) y z -> (b u) c (y z)", u=HALVES)
+        for r in range(X_LOADS):
+            nc.scalar.dma_start(
+                out=x_raw[r * BATCH * HALVES : (r + 1) * BATCH * HALVES], in_=x_rows
+            )
         bias_rows = keep.tile([BATCH, OUT_CH, LOCATIONS], BF16)
         nc.scalar.dma_start(
             out=bias_rows[:].rearrange("b o l -> b (o l)"),
             in_=bias.rearrange("o h w -> (o h w)").partition_broadcast(BATCH),
         )
-        w_loads = weights.rearrange(
-            "h w (g o) (t c) i j -> (h w g) (o t) c i j", o=O_LOAD, t=PACK
-        )
-        w_raw = []
-        for n in range(UNITS * LOADS_PER_UNIT):
-            w_tile = w_pool.tile([P, P, TAPS, TAPS], BF16, name="w_tile")
-            nc.sync.dma_start(out=w_tile[:], in_=w_loads[n])
-            w_raw.append(w_tile)
+        w_halves = weights.rearrange("h w o (u c) i j -> (h w) u o c i j", u=HALVES)
+        w_raw = {}
+        for loc in range(LOCATIONS):
+            for u in range(HALVES):
+                w_tile = w_pool.tile([P, C_HALF, TAPS, TAPS], BF16, name="w_tile")
+                nc.sync.dma_start(out=w_tile[:], in_=w_halves[loc, u])
+                w_raw[(loc, u)] = w_tile
 
-        identity = keep.tile([P, P], BF16)
+        identity = keep.tile([P, P], F32)
         make_identity(nc, identity[:])
 
-        x_t = psum_x.tile([P, PIXELS, P], BF16)
-        for q in range(PIXELS):
-            nc.tensor.transpose(x_t[:, q, :], x_raw[:, :, q], identity[:])
-        x_grouped = keep.tile([P, PIXELS, COPIES, P], BF16, align_bytes=64)
-        nc.scalar.copy(
-            out=x_grouped[:],
-            in_=x_t[:].unsqueeze(2).to_broadcast([P, PIXELS, COPIES, P]),
-        )
+        x_sorted = keep.tile([P, PIXELS, C_HALF], BF16)
+        x_t = psum_x.tile([P, PIXELS, P], F32)
+        x_grouped = keep.tile([P, PIXELS, X_REPEATS, P * PAIR], BF16, align_bytes=64)
         x_codes = keep.tile([P, PIXELS, P], U32, align_bytes=64)
         x_scales = keep.tile([P, PIXELS, P], U8, align_bytes=64)
-        nc.vector.quantize_mx(
-            out=x_codes[:].rearrange("p q m -> p (q m)").bitcast(FP8X4),
-            scales=x_scales[:].rearrange("p q m -> p (q m)"),
-            in_=x_grouped[:].rearrange("p q r m -> p (q r m)"),
-        )
 
-        w_codes = keep.tile([P, PIXELS, LOCATIONS, OUT_CH], U32, align_bytes=64)
-        w_scales = keep.tile([P, PIXELS, LOCATIONS, OUT_CH], U8, align_bytes=64)
+        def sort_x():
+            nc.scalar.copy(out=x_sorted[:], in_=x_raw[:].rearrange("p c q -> p q c"))
+
+        def transpose_x():
+            for q in range(PIXELS):
+                nc.tensor.transpose(x_t[:, q, :], x_sorted[:, q, :].bitcast(F32), identity[:])
+
+        def quantise_x():
+            nc.vector.tensor_copy(
+                out=x_grouped[:].bitcast(F32),
+                in_=x_t[:].unsqueeze(2).to_broadcast([P, PIXELS, X_REPEATS, P]),
+            )
+            nc.vector.quantize_mx(
+                out=x_codes[:].rearrange("p q m -> p (q m)").bitcast(FP8X4),
+                scales=x_scales[:].rearrange("p q m -> p (q m)"),
+                in_=x_grouped[:].rearrange("p q r m -> p (q r m)"),
+            )
+
+        w_codes = keep.tile([P, LOCATIONS, PIXELS, OUT_CH], U32, align_bytes=64)
+        w_scales = keep.tile([P, LOCATIONS, PIXELS, OUT_CH], U8, align_bytes=64)
         acc = psum_acc.tile([P, LOCATIONS, OUT_CH], F32)
+        w_t = {}
+        w_grouped = {}
 
-        for loc in range(LOCATIONS):
+        def sort_and_transpose(loc, u):
             h, w = divmod(loc, SIDE)
-            for half in range(UNITS_PER_LOCATION):
-                o_cols = slice(half * O_UNIT, (half + 1) * O_UNIT)
-                w_picked = stage.tile([P, LOADS_PER_UNIT, SIDE, P, SIDE], BF16)
-                for s in range(LOADS_PER_UNIT):
-                    w_tile = w_raw[(loc * UNITS_PER_LOCATION + half) * LOADS_PER_UNIT + s]
-                    nc.vector.tensor_copy(
-                        out=w_picked[:, s],
-                        in_=w_tile[:, :, 1 - h : 1 - h + SIDE, 1 - w : 1 - w + SIDE].rearrange(
-                            "p c y z -> p y c z"
-                        ),
+            for y in range(SIDE):
+                taps = w_raw[(loc, u)][:, :, y - h + 1, 1 - w : 1 - w + SIDE]
+                w_sorted = stage.tile([P, SIDE, C_HALF], BF16)
+                by_channel = w_sorted[:].rearrange("p z c -> p c z")
+                nc.vector.tensor_copy(out=by_channel[:, :C_VECTOR], in_=taps[:, :C_VECTOR])
+                nc.scalar.copy(out=by_channel[:, C_VECTOR:], in_=taps[:, C_VECTOR:])
+                if u == 0:
+                    w_t[(loc, y)] = psum_t.tile([P, SIDE, HALVES, OUT_CH], F32, name="w_t")
+                for z in range(SIDE):
+                    nc.tensor.transpose(
+                        w_t[(loc, y)][:, z, u, :], w_sorted[:, z, :].bitcast(F32), identity[:]
                     )
-                for q in range(PIXELS):
-                    y, z = divmod(q, SIDE)
-                    w_t = psum_t.tile([P, LOADS_PER_UNIT, P], BF16)
-                    for s in range(LOADS_PER_UNIT):
-                        nc.tensor.transpose(w_t[:, s, :], w_picked[:, s, y, :, z], identity[:])
-                    w_grouped = stage.tile([P, O_UNIT * PACK], BF16, align_bytes=64)
-                    nc.scalar.copy(out=w_grouped[:], in_=w_t[:].rearrange("p s m -> p (s m)"))
-                    nc.vector.quantize_mx(
-                        out=w_codes[:, q, loc, o_cols].bitcast(FP8X4),
-                        scales=w_scales[:, q, loc, o_cols],
-                        in_=w_grouped[:],
-                    )
+
+        def regroup(loc):
+            for y in range(SIDE):
+                w_grouped[(loc, y)] = stage.tile(
+                    [P, SIDE, OUT_CH, PACK], BF16, align_bytes=64, name="w_grouped"
+                )
+                nc.scalar.copy(
+                    out=w_grouped[(loc, y)][:].bitcast(F32),
+                    in_=w_t[(loc, y)][:].rearrange("p z u o -> p z o u"),
+                )
+
+        def quantise_and_multiply(loc):
+            for y in range(SIDE):
+                pixels = slice(y * SIDE, (y + 1) * SIDE)
+                nc.vector.quantize_mx(
+                    out=w_codes[:, loc, pixels, :].rearrange("p q o -> p (q o)").bitcast(FP8X4),
+                    scales=w_scales[:, loc, pixels, :].rearrange("p q o -> p (q o)"),
+                    in_=w_grouped[(loc, y)][:].rearrange("p z o t -> p (z o t)"),
+                )
             for q in range(PIXELS):
                 nc.tensor.matmul_mx(
                     out=acc[:, loc, :],
                     lhsT=x_codes[:, q, :].bitcast(FP8X4),
                     lhsT_scale=x_scales[:, q, :],
-                    rhs=w_codes[:, q, loc, :].bitcast(FP8X4),
-                    rhs_scale=w_scales[:, q, loc, :],
+                    rhs=w_codes[:, loc, q, :].bitcast(FP8X4),
+                    rhs_scale=w_scales[:, loc, q, :],
                     start=(q == 0),
                     stop=(q == PIXELS - 1),
                 )
+
+        for loc in range(LOCATIONS):
+            sort_and_transpose(loc, 0)
+            if loc == 0:
+                sort_x()
+                transpose_x()
+            else:
+                quantise_and_multiply(loc - 1)
+            sort_and_transpose(loc, 1)
+            if loc == 0:
+                quantise_x()
+            regroup(loc)
+        quantise_and_multiply(LOCATIONS - 1)
 
         result = keep.tile([BATCH, OUT_CH, LOCATIONS], F32)
         nc.vector.tensor_tensor(

@@ -21,9 +21,14 @@ SIDE = 2
 TAPS = 3
 PIXELS = SIDE * SIDE
 LOCATIONS = SIDE * SIDE
+O_UNIT = P // HALVES
+UNITS_PER_LOCATION = OUT_CH // O_UNIT
+UNITS = LOCATIONS * UNITS_PER_LOCATION
 X_LOADS = P // (BATCH * HALVES)
-X_REPEATS = P // (X_LOADS * BATCH)
-C_VECTOR = 3 * C_HALF // 4
+X_COLS = X_LOADS * BATCH
+STEPS = UNITS * SIDE
+STEPS_PER_LOCATION = STEPS // LOCATIONS
+C_VECTOR = 13 * C_HALF // 16
 
 FLOPS = 2 * BATCH * OUT_CH * LOCATIONS * PIXELS * CHANNELS
 BYTES = (
@@ -38,17 +43,16 @@ def tile_locallyconnected2d_s_kernel(tc, x, weights, bias, out):
     nc = tc.nc
     with ExitStack() as stack:
         keep = stack.enter_context(tc.tile_pool(name="keep", bufs=1))
-        w_pool = stack.enter_context(tc.tile_pool(name="w_pool", bufs=LOCATIONS * HALVES))
+        w_pool = stack.enter_context(tc.tile_pool(name="w_pool", bufs=UNITS))
         stage = stack.enter_context(tc.tile_pool(name="stage", bufs=4))
-        psum_t = stack.enter_context(tc.psum_pool(name="psum_t", bufs=2 * SIDE))
+        psum_t = stack.enter_context(tc.psum_pool(name="psum_t", bufs=4))
         psum_x = stack.enter_context(tc.psum_pool(name="psum_x", bufs=1))
         psum_acc = stack.enter_context(tc.psum_pool(name="psum_acc", bufs=1))
-        stack.enter_context(tc.manual_schedule())
 
         x_raw = keep.tile([P, C_HALF, PIXELS], BF16)
         x_rows = x.rearrange("b (u c) y z -> (b u) c (y z)", u=HALVES)
         for r in range(X_LOADS):
-            nc.scalar.dma_start(
+            nc.sync.dma_start(
                 out=x_raw[r * BATCH * HALVES : (r + 1) * BATCH * HALVES], in_=x_rows
             )
         bias_rows = keep.tile([BATCH, OUT_CH, LOCATIONS], BF16)
@@ -56,103 +60,109 @@ def tile_locallyconnected2d_s_kernel(tc, x, weights, bias, out):
             out=bias_rows[:].rearrange("b o l -> b (o l)"),
             in_=bias.rearrange("o h w -> (o h w)").partition_broadcast(BATCH),
         )
-        w_halves = weights.rearrange("h w o (u c) i j -> (h w) u o c i j", u=HALVES)
-        w_raw = {}
-        for loc in range(LOCATIONS):
-            for u in range(HALVES):
-                w_tile = w_pool.tile([P, C_HALF, TAPS, TAPS], BF16, name="w_tile")
-                nc.sync.dma_start(out=w_tile[:], in_=w_halves[loc, u])
-                w_raw[(loc, u)] = w_tile
+        w_loads = weights.rearrange(
+            "h w (g o) (u c) i j -> (h w g) (o u) c i j", o=O_UNIT, u=HALVES
+        )
+        w_raw = []
+        for n in range(UNITS):
+            w_tile = w_pool.tile([P, C_HALF, TAPS, TAPS], BF16, name="w_tile")
+            nc.sync.dma_start(out=w_tile[:], in_=w_loads[n])
+            w_raw.append(w_tile)
 
         identity = keep.tile([P, P], F32)
         make_identity(nc, identity[:])
 
         x_sorted = keep.tile([P, PIXELS, C_HALF], BF16)
         x_t = psum_x.tile([P, PIXELS, P], F32)
-        x_grouped = keep.tile([P, PIXELS, X_REPEATS, P * PAIR], BF16, align_bytes=64)
+        x_grouped = keep.tile([P, PIXELS, P, PACK], BF16, align_bytes=64)
         x_codes = keep.tile([P, PIXELS, P], U32, align_bytes=64)
         x_scales = keep.tile([P, PIXELS, P], U8, align_bytes=64)
 
+        nc.vector.memset(x_grouped[:].bitcast(F32), 0.0)
+
         def sort_x():
-            nc.scalar.copy(out=x_sorted[:], in_=x_raw[:].rearrange("p c q -> p q c"))
+            nc.vector.tensor_copy(out=x_sorted[:], in_=x_raw[:].rearrange("p c q -> p q c"))
 
         def transpose_x():
             for q in range(PIXELS):
                 nc.tensor.transpose(x_t[:, q, :], x_sorted[:, q, :].bitcast(F32), identity[:])
 
-        def quantise_x():
-            nc.vector.tensor_copy(
-                out=x_grouped[:].bitcast(F32),
-                in_=x_t[:].unsqueeze(2).to_broadcast([P, PIXELS, X_REPEATS, P]),
+        def regroup_x():
+            nc.scalar.copy(
+                out=x_grouped[:, :, :X_COLS, :].rearrange("p q m t -> p q (m t)").bitcast(F32),
+                in_=x_t[:],
             )
+
+        def quantise_x():
             nc.vector.quantize_mx(
                 out=x_codes[:].rearrange("p q m -> p (q m)").bitcast(FP8X4),
                 scales=x_scales[:].rearrange("p q m -> p (q m)"),
-                in_=x_grouped[:].rearrange("p q r m -> p (q r m)"),
+                in_=x_grouped[:].rearrange("p q m t -> p (q m t)"),
             )
 
-        w_codes = keep.tile([P, LOCATIONS, PIXELS, OUT_CH], U32, align_bytes=64)
-        w_scales = keep.tile([P, LOCATIONS, PIXELS, OUT_CH], U8, align_bytes=64)
+        w_codes = keep.tile([P, PIXELS, LOCATIONS, OUT_CH], U32, align_bytes=64)
+        w_scales = keep.tile([P, PIXELS, LOCATIONS, OUT_CH], U8, align_bytes=64)
         acc = psum_acc.tile([P, LOCATIONS, OUT_CH], F32)
+        w_sorted = {}
         w_t = {}
         w_grouped = {}
 
-        def sort_and_transpose(loc, u):
-            h, w = divmod(loc, SIDE)
-            for y in range(SIDE):
-                taps = w_raw[(loc, u)][:, :, y - h + 1, 1 - w : 1 - w + SIDE]
-                w_sorted = stage.tile([P, SIDE, C_HALF], BF16)
-                by_channel = w_sorted[:].rearrange("p z c -> p c z")
-                nc.vector.tensor_copy(out=by_channel[:, :C_VECTOR], in_=taps[:, :C_VECTOR])
-                nc.scalar.copy(out=by_channel[:, C_VECTOR:], in_=taps[:, C_VECTOR:])
-                if u == 0:
-                    w_t[(loc, y)] = psum_t.tile([P, SIDE, HALVES, OUT_CH], F32, name="w_t")
-                for z in range(SIDE):
-                    nc.tensor.transpose(
-                        w_t[(loc, y)][:, z, u, :], w_sorted[:, z, :].bitcast(F32), identity[:]
-                    )
+        def sort_taps(step):
+            n, y = divmod(step, SIDE)
+            h, w = divmod(n // UNITS_PER_LOCATION, SIDE)
+            taps = w_raw[n][:, :, y - h + 1, 1 - w : 1 - w + SIDE]
+            w_sorted[step] = stage.tile([P, SIDE, C_HALF], BF16, name="w_sorted")
+            by_channel = w_sorted[step][:].rearrange("p z c -> p c z")
+            nc.vector.tensor_copy(out=by_channel[:, :C_VECTOR], in_=taps[:, :C_VECTOR])
+            nc.scalar.copy(out=by_channel[:, C_VECTOR:], in_=taps[:, C_VECTOR:])
 
-        def regroup(loc):
-            for y in range(SIDE):
-                w_grouped[(loc, y)] = stage.tile(
-                    [P, SIDE, OUT_CH, PACK], BF16, align_bytes=64, name="w_grouped"
-                )
-                nc.scalar.copy(
-                    out=w_grouped[(loc, y)][:].bitcast(F32),
-                    in_=w_t[(loc, y)][:].rearrange("p z u o -> p z o u"),
+        def transpose_taps(step):
+            w_t[step] = psum_t.tile([P, SIDE, P], F32, name="w_t")
+            for z in range(SIDE):
+                nc.tensor.transpose(
+                    w_t[step][:, z, :], w_sorted[step][:, z, :].bitcast(F32), identity[:]
                 )
 
-        def quantise_and_multiply(loc):
-            for y in range(SIDE):
-                pixels = slice(y * SIDE, (y + 1) * SIDE)
+        def regroup(step):
+            w_grouped[step] = stage.tile(
+                [P, SIDE, O_UNIT * PACK], BF16, align_bytes=64, name="w_grouped"
+            )
+            nc.scalar.copy(out=w_grouped[step][:].bitcast(F32), in_=w_t[step][:])
+
+        def quantise(step):
+            n, y = divmod(step, SIDE)
+            loc, half = divmod(n, UNITS_PER_LOCATION)
+            o_cols = slice(half * O_UNIT, (half + 1) * O_UNIT)
+            for z in range(SIDE):
                 nc.vector.quantize_mx(
-                    out=w_codes[:, loc, pixels, :].rearrange("p q o -> p (q o)").bitcast(FP8X4),
-                    scales=w_scales[:, loc, pixels, :].rearrange("p q o -> p (q o)"),
-                    in_=w_grouped[(loc, y)][:].rearrange("p z o t -> p (z o t)"),
+                    out=w_codes[:, y * SIDE + z, loc, o_cols].bitcast(FP8X4),
+                    scales=w_scales[:, y * SIDE + z, loc, o_cols],
+                    in_=w_grouped[step][:, z, :],
                 )
+
+        def multiply(loc):
             for q in range(PIXELS):
                 nc.tensor.matmul_mx(
                     out=acc[:, loc, :],
                     lhsT=x_codes[:, q, :].bitcast(FP8X4),
                     lhsT_scale=x_scales[:, q, :],
-                    rhs=w_codes[:, loc, q, :].bitcast(FP8X4),
-                    rhs_scale=w_scales[:, loc, q, :],
+                    rhs=w_codes[:, q, loc, :].bitcast(FP8X4),
+                    rhs_scale=w_scales[:, q, loc, :],
                     start=(q == 0),
                     stop=(q == PIXELS - 1),
                 )
 
-        for loc in range(LOCATIONS):
-            sort_and_transpose(loc, 0)
-            if loc == 0:
-                sort_x()
-                transpose_x()
-            else:
-                quantise_and_multiply(loc - 1)
-            sort_and_transpose(loc, 1)
-            if loc == 0:
-                quantise_x()
-            regroup(loc)
-        quantise_and_multiply(LOCATIONS - 1)
+        sort_x()
+        transpose_x()
+        regroup_x()
+        quantise_x()
+        for step in range(STEPS):
+            sort_taps(step)
+            transpose_taps(step)
+            regroup(step)
+            quantise(step)
+            if step % STEPS_PER_LOCATION == STEPS_PER_LOCATION - 1:
+                multiply(step // STEPS_PER_LOCATION)
 
         result = keep.tile([BATCH, OUT_CH, LOCATIONS], F32)
         nc.vector.tensor_tensor(

@@ -43,7 +43,7 @@ def tile_locallyconnected2d_s_kernel(tc, x, weights, bias, out):
     nc = tc.nc
     with ExitStack() as stack:
         keep = stack.enter_context(tc.tile_pool(name="keep", bufs=1))
-        w_pool = stack.enter_context(tc.tile_pool(name="w_pool", bufs=UNITS))
+        w_pool = stack.enter_context(tc.tile_pool(name="w_pool", bufs=LOCATIONS))
         stage = stack.enter_context(tc.tile_pool(name="stage", bufs=4))
         psum_t = stack.enter_context(tc.psum_pool(name="psum_t", bufs=4))
         psum_x = stack.enter_context(tc.psum_pool(name="psum_x", bufs=1))
@@ -60,14 +60,18 @@ def tile_locallyconnected2d_s_kernel(tc, x, weights, bias, out):
             out=bias_rows[:].rearrange("b o l -> b (o l)"),
             in_=bias.rearrange("o h w -> (o h w)").partition_broadcast(BATCH),
         )
-        w_loads = weights.rearrange(
-            "h w (g o) (u c) i j -> (h w g) (o u) c i j", o=O_UNIT, u=HALVES
+        w_units = weights.rearrange(
+            "h w (g o) (u c) i j -> (h w) (o u) g c i j", o=O_UNIT, u=HALVES
         )
         w_raw = []
-        for n in range(UNITS):
-            w_tile = w_pool.tile([P, C_HALF, TAPS, TAPS], BF16, name="w_tile")
-            nc.sync.dma_start(out=w_tile[:], in_=w_loads[n])
-            w_raw.append(w_tile)
+        for loc in range(LOCATIONS):
+            w_tile = w_pool.tile([P, UNITS_PER_LOCATION, C_HALF, TAPS, TAPS], BF16, name="w_tile")
+            if loc < LOCATIONS - 1:
+                nc.sync.dma_start(out=w_tile[:], in_=w_units[loc])
+            else:
+                for g in range(UNITS_PER_LOCATION):
+                    nc.sync.dma_start(out=w_tile[:, g], in_=w_units[loc][:, g])
+            w_raw.extend([w_tile[:, g] for g in range(UNITS_PER_LOCATION)])
 
         identity = keep.tile([P, P], F32)
         make_identity(nc, identity[:])

@@ -43,11 +43,12 @@ def tile_locallyconnected2d_s_kernel(tc, x, weights, bias, out):
     nc = tc.nc
     with ExitStack() as stack:
         keep = stack.enter_context(tc.tile_pool(name="keep", bufs=1))
-        w_pool = stack.enter_context(tc.tile_pool(name="w_pool", bufs=LOCATIONS))
+        w_pool = stack.enter_context(tc.tile_pool(name="w_pool", bufs=UNITS))
         stage = stack.enter_context(tc.tile_pool(name="stage", bufs=4))
         psum_t = stack.enter_context(tc.psum_pool(name="psum_t", bufs=4))
         psum_x = stack.enter_context(tc.psum_pool(name="psum_x", bufs=1))
         psum_acc = stack.enter_context(tc.psum_pool(name="psum_acc", bufs=1))
+        psum_unread = stack.enter_context(tc.psum_pool(name="psum_unread", bufs=1))
 
         x_raw = keep.tile([P, C_HALF, PIXELS], BF16)
         x_rows = x.rearrange("b (u c) y z -> (b u) c (y z)", u=HALVES)
@@ -60,18 +61,14 @@ def tile_locallyconnected2d_s_kernel(tc, x, weights, bias, out):
             out=bias_rows[:].rearrange("b o l -> b (o l)"),
             in_=bias.rearrange("o h w -> (o h w)").partition_broadcast(BATCH),
         )
-        w_units = weights.rearrange(
-            "h w (g o) (u c) i j -> (h w) (o u) g c i j", o=O_UNIT, u=HALVES
+        w_loads = weights.rearrange(
+            "h w (g o) (u c) i j -> (h w g) (o u) c i j", o=O_UNIT, u=HALVES
         )
         w_raw = []
-        for loc in range(LOCATIONS):
-            w_tile = w_pool.tile([P, UNITS_PER_LOCATION, C_HALF, TAPS, TAPS], BF16, name="w_tile")
-            if loc < LOCATIONS - 1:
-                nc.sync.dma_start(out=w_tile[:], in_=w_units[loc])
-            else:
-                for g in range(UNITS_PER_LOCATION):
-                    nc.sync.dma_start(out=w_tile[:, g], in_=w_units[loc][:, g])
-            w_raw.extend([w_tile[:, g] for g in range(UNITS_PER_LOCATION)])
+        for n in range(UNITS):
+            w_tile = w_pool.tile([P, C_HALF, TAPS, TAPS], BF16, name="w_tile")
+            nc.sync.dma_start(out=w_tile[:], in_=w_loads[n])
+            w_raw.append(w_tile)
 
         identity = keep.tile([P, P], F32)
         make_identity(nc, identity[:])
@@ -107,6 +104,7 @@ def tile_locallyconnected2d_s_kernel(tc, x, weights, bias, out):
         w_codes = keep.tile([P, PIXELS, LOCATIONS, OUT_CH], U32, align_bytes=64)
         w_scales = keep.tile([P, PIXELS, LOCATIONS, OUT_CH], U8, align_bytes=64)
         acc = psum_acc.tile([P, LOCATIONS, OUT_CH], F32)
+        unread = psum_unread.tile([P, P], F32)
         w_sorted = {}
         w_t = {}
         w_grouped = {}
@@ -126,6 +124,7 @@ def tile_locallyconnected2d_s_kernel(tc, x, weights, bias, out):
                 nc.tensor.transpose(
                     w_t[step][:, z, :], w_sorted[step][:, z, :].bitcast(F32), identity[:]
                 )
+            nc.tensor.transpose(unread[:], w_sorted[step][:, 0, :].bitcast(F32), identity[:])
 
         def regroup(step):
             w_grouped[step] = stage.tile(

from contextlib import ExitStack

import concourse.mybir as mybir
from concourse.masks import make_identity

BF16 = mybir.dt.bfloat16
F32 = mybir.dt.float32
U32 = mybir.dt.uint32
U8 = mybir.dt.uint8
FP8X4 = mybir.dt.float8_e4m3fn_x4

P = 128
PACK = 4
PAIR = 2
BATCH = 32
CHANNELS = P * PACK
HALVES = PACK // PAIR
C_HALF = CHANNELS // HALVES
OUT_CH = 128
SIDE = 2
TAPS = 3
PIXELS = SIDE * SIDE
LOCATIONS = SIDE * SIDE
O_UNIT = P // HALVES
UNITS_PER_LOCATION = OUT_CH // O_UNIT
UNITS = LOCATIONS * UNITS_PER_LOCATION
X_LOADS = P // (BATCH * HALVES)
X_COLS = X_LOADS * BATCH
STEPS = UNITS * SIDE
STEPS_PER_LOCATION = STEPS // LOCATIONS
C_VECTOR = 13 * C_HALF // 16

FLOPS = 2 * BATCH * OUT_CH * LOCATIONS * PIXELS * CHANNELS
BYTES = (
    2 * BATCH * CHANNELS * PIXELS
    + 2 * LOCATIONS * OUT_CH * CHANNELS * PIXELS
    + 2 * OUT_CH * LOCATIONS
    + 4 * BATCH * OUT_CH * LOCATIONS
)


def tile_locallyconnected2d_s_kernel(tc, x, weights, bias, out):
    nc = tc.nc
    with ExitStack() as stack:
        keep = stack.enter_context(tc.tile_pool(name="keep", bufs=1))
        w_pool = stack.enter_context(tc.tile_pool(name="w_pool", bufs=UNITS))
        stage = stack.enter_context(tc.tile_pool(name="stage", bufs=4))
        psum_t = stack.enter_context(tc.psum_pool(name="psum_t", bufs=4))
        psum_x = stack.enter_context(tc.psum_pool(name="psum_x", bufs=1))
        psum_acc = stack.enter_context(tc.psum_pool(name="psum_acc", bufs=1))
        psum_unread = stack.enter_context(tc.psum_pool(name="psum_unread", bufs=1))

        x_raw = keep.tile([P, C_HALF, PIXELS], BF16)
        x_rows = x.rearrange("b (u c) y z -> (b u) c (y z)", u=HALVES)
        for r in range(X_LOADS):
            nc.sync.dma_start(
                out=x_raw[r * BATCH * HALVES : (r + 1) * BATCH * HALVES], in_=x_rows
            )
        bias_rows = keep.tile([BATCH, OUT_CH, LOCATIONS], BF16)
        nc.scalar.dma_start(
            out=bias_rows[:].rearrange("b o l -> b (o l)"),
            in_=bias.rearrange("o h w -> (o h w)").partition_broadcast(BATCH),
        )
        w_loads = weights.rearrange(
            "h w (g o) (u c) i j -> (h w g) (o u) c i j", o=O_UNIT, u=HALVES
        )
        w_raw = []
        for n in range(UNITS):
            w_tile = w_pool.tile([P, C_HALF, TAPS, TAPS], BF16, name="w_tile")
            nc.sync.dma_start(out=w_tile[:], in_=w_loads[n])
            w_raw.append(w_tile)

        identity = keep.tile([P, P], F32)
        make_identity(nc, identity[:])

        x_sorted = keep.tile([P, PIXELS, C_HALF], BF16)
        x_t = psum_x.tile([P, PIXELS, P], F32)
        x_grouped = keep.tile([P, PIXELS, P, PACK], BF16, align_bytes=64)
        x_codes = keep.tile([P, PIXELS, P], U32, align_bytes=64)
        x_scales = keep.tile([P, PIXELS, P], U8, align_bytes=64)

        nc.vector.memset(x_grouped[:].bitcast(F32), 0.0)

        def sort_x():
            nc.vector.tensor_copy(out=x_sorted[:], in_=x_raw[:].rearrange("p c q -> p q c"))

        def transpose_x():
            for q in range(PIXELS):
                nc.tensor.transpose(x_t[:, q, :], x_sorted[:, q, :].bitcast(F32), identity[:])

        def regroup_x():
            nc.scalar.copy(
                out=x_grouped[:, :, :X_COLS, :].rearrange("p q m t -> p q (m t)").bitcast(F32),
                in_=x_t[:],
            )

        def quantise_x():
            nc.vector.quantize_mx(
                out=x_codes[:].rearrange("p q m -> p (q m)").bitcast(FP8X4),
                scales=x_scales[:].rearrange("p q m -> p (q m)"),
                in_=x_grouped[:].rearrange("p q m t -> p (q m t)"),
            )

        w_codes = keep.tile([P, PIXELS, LOCATIONS, OUT_CH], U32, align_bytes=64)
        w_scales = keep.tile([P, PIXELS, LOCATIONS, OUT_CH], U8, align_bytes=64)
        acc = psum_acc.tile([P, LOCATIONS, OUT_CH], F32)
        unread = psum_unread.tile([P, P], F32)
        w_sorted = {}
        w_t = {}
        w_grouped = {}

        def sort_taps(step):
            n, y = divmod(step, SIDE)
            h, w = divmod(n // UNITS_PER_LOCATION, SIDE)
            taps = w_raw[n][:, :, y - h + 1, 1 - w : 1 - w + SIDE]
            w_sorted[step] = stage.tile([P, SIDE, C_HALF], BF16, name="w_sorted")
            by_channel = w_sorted[step][:].rearrange("p z c -> p c z")
            nc.vector.tensor_copy(out=by_channel[:, :C_VECTOR], in_=taps[:, :C_VECTOR])
            nc.scalar.copy(out=by_channel[:, C_VECTOR:], in_=taps[:, C_VECTOR:])

        def transpose_taps(step):
            w_t[step] = psum_t.tile([P, SIDE, P], F32, name="w_t")
            for z in range(SIDE):
                nc.tensor.transpose(
                    w_t[step][:, z, :], w_sorted[step][:, z, :].bitcast(F32), identity[:]
                )
            nc.tensor.transpose(unread[:], w_sorted[step][:, 0, :].bitcast(F32), identity[:])

        def regroup(step):
            w_grouped[step] = stage.tile(
                [P, SIDE, O_UNIT * PACK], BF16, align_bytes=64, name="w_grouped"
            )
            nc.scalar.copy(out=w_grouped[step][:].bitcast(F32), in_=w_t[step][:])

        def quantise(step):
            n, y = divmod(step, SIDE)
            loc, half = divmod(n, UNITS_PER_LOCATION)
            o_cols = slice(half * O_UNIT, (half + 1) * O_UNIT)
            for z in range(SIDE):
                nc.vector.quantize_mx(
                    out=w_codes[:, y * SIDE + z, loc, o_cols].bitcast(FP8X4),
                    scales=w_scales[:, y * SIDE + z, loc, o_cols],
                    in_=w_grouped[step][:, z, :],
                )

        def multiply(loc):
            for q in range(PIXELS):
                nc.tensor.matmul_mx(
                    out=acc[:, loc, :],
                    lhsT=x_codes[:, q, :].bitcast(FP8X4),
                    lhsT_scale=x_scales[:, q, :],
                    rhs=w_codes[:, q, loc, :].bitcast(FP8X4),
                    rhs_scale=w_scales[:, q, loc, :],
                    start=(q == 0),
                    stop=(q == PIXELS - 1),
                )

        sort_x()
        transpose_x()
        regroup_x()
        quantise_x()
        for step in range(STEPS):
            sort_taps(step)
            transpose_taps(step)
            regroup(step)
            quantise(step)
            if step % STEPS_PER_LOCATION == STEPS_PER_LOCATION - 1:
                multiply(step // STEPS_PER_LOCATION)

        result = keep.tile([BATCH, OUT_CH, LOCATIONS], F32)
        nc.vector.tensor_tensor(
            out=result[:],
            in0=acc[0:BATCH].rearrange("b l o -> b o l"),
            in1=bias_rows[:],
            op=mybir.AluOpType.add,
        )
        nc.sync.dma_start(
            out=out.rearrange("b o h w -> b (o h w)"),
            in_=result[:].rearrange("b o l -> b (o l)"),
        )
